import numpy as np
import ml_dtypes


def mxq(x, axis, fmt="e4m3"):
    dtype, down = {"e4m3": (ml_dtypes.float8_e4m3fn, 7), "e5m2": (ml_dtypes.float8_e5m2, 14)}[fmt]
    v = np.moveaxis(np.asarray(x, np.float32).astype(ml_dtypes.bfloat16).astype(np.float64), axis, -1)
    blocks = v.reshape(v.shape[:-1] + (-1, 32))
    amax = np.abs(blocks).max(-1, keepdims=True)
    byte = np.maximum(np.where(amax > 0, np.frexp(amax)[1] - 1 + 127, 0) - down, 1)
    scale = np.exp2(byte - 127.0)
    codes = (blocks / scale).astype(np.float32).astype(dtype).astype(np.float64)
    return np.moveaxis((codes * scale).reshape(v.shape), -1, axis)


WIDE = False


def mx_kscale(k):
    if not WIDE:
        return np.ones(k)
    levels = np.array([10, -10, 5, -5, 0])
    a = np.random.permutation(np.resize(levels, k // 512 * 4)).reshape(k // 512, 4)
    idx = np.arange(k)
    return np.exp2(a[idx // 512, idx % 128 // 32])


BF16 = ml_dtypes.bfloat16


def bf(x):
    return np.asarray(x, np.float32).astype(BF16)


def f64(x):
    return np.asarray(x).astype(np.float64)


N, K, D_IN, HC, H = 256, 8, 1024, 1024, 1024


def sigmoid(v):
    return 1.0 / (1.0 + np.exp(-v))


def setup_inputs():
    s, t = mx_kscale(D_IN), mx_kscale(HC)
    d = {
        "x": bf(np.random.standard_normal((N, D_IN)) * s),
        "child_h": bf(np.random.standard_normal((N, K, HC)) * t),
        "fc_sum": bf(np.random.standard_normal((N, H)) * 0.27 * np.sqrt(K)),
    }
    for g in ("i", "o", "u"):
        d["W" + g] = bf(np.random.standard_normal((D_IN, H)) * 0.7 / np.sqrt(D_IN) / s[:, None])
        d["bW" + g] = bf(np.random.standard_normal(H) * 0.3)
        d["U" + g] = bf(np.random.standard_normal((HC, H)) * 0.7 / np.sqrt(K * HC) / t[:, None])
        d["bU" + g] = bf(np.random.standard_normal(H) * 0.3)
    return d


def reference(x, child_h, fc_sum, Wi, bWi, Ui, bUi, Wo, bWo, Uo, bUo, Wu, bWu, Uu, bUu):
    h_sum = f64(child_h).sum(axis=1)
    xq = mxq(f64(x), 1, "e4m3")
    hq = mxq(h_sum, 1, "e4m3")
    i = sigmoid((xq @ mxq(f64(Wi), 0, "e4m3")) + f64(bWi) + (hq @ mxq(f64(Ui), 0, "e4m3")) + f64(bUi))
    o = sigmoid((xq @ mxq(f64(Wo), 0, "e4m3")) + f64(bWo) + (hq @ mxq(f64(Uo), 0, "e4m3")) + f64(bUo))
    u = np.tanh((xq @ mxq(f64(Wu), 0, "e4m3")) + f64(bWu) + (hq @ mxq(f64(Uu), 0, "e4m3")) + f64(bUu))
    c = i * u + f64(fc_sum)
    h = o * np.tanh(c)
    return np.stack([h, c], axis=0)

@@ -1,0 +1,239 @@
+from contextlib import ExitStack
+
+import concourse.mybir as mybir
+from concourse.masks import make_identity
+
+F32 = mybir.dt.float32
+BF16 = mybir.dt.bfloat16
+U32 = mybir.dt.uint32
+U8 = mybir.dt.uint8
+FP8X4 = mybir.dt.float8_e4m3fn_x4
+ACT = mybir.ActivationFunctionType
+ALU = mybir.AluOpType
+
+P = 128
+PACK = 4
+K_PASS = P * PACK
+NODES = 256
+NODE_TILES = NODES // P
+CHILDREN = 8
+FEATURES = 1024
+PASSES = FEATURES // K_PASS
+HIDDEN = 1024
+COL_TILES = HIDDEN // P
+BANK = 512
+
+ROWS_PER_PARTITION = 2
+NODES_PER_LOAD = P * ROWS_PER_PARTITION // CHILDREN
+PARTITIONS_PER_NODE = P // NODES_PER_LOAD
+CHILD_LOADS = NODES // NODES_PER_LOAD
+
+GATE_I, GATE_U, GATE_O = 0, 1, 2
+
+VECTOR_COLS = 512
+
+FLOPS = 2 * NODES * FEATURES * HIDDEN * 6
+
+
+def tile_childsumtreelstmcell_pb_kernel(
+    tc, x, child_h, fc_sum, Wi, bWi, Ui, bUi, Wo, bWo, Uo, bUo, Wu, bWu, Uu, bUu, out
+):
+    nc = tc.nc
+    with ExitStack() as ctx:
+        const = ctx.enter_context(tc.tile_pool(name="const", bufs=1))
+        keep = ctx.enter_context(tc.tile_pool(name="keep", bufs=1))
+        raw_pool = ctx.enter_context(tc.tile_pool(name="raw", bufs=6))
+        grouped_pool = ctx.enter_context(tc.tile_pool(name="grouped", bufs=3))
+        child_pool = ctx.enter_context(tc.tile_pool(name="child", bufs=4))
+        psum = ctx.enter_context(tc.psum_pool(name="psum", bufs=8))
+
+        ident = const.tile([P, P], F32)
+        make_identity(nc, ident[:])
+        node_of_f32 = const.tile([P, NODES_PER_LOAD], F32)
+        nc.vector.reduce_sum(
+            out=node_of_f32[:],
+            in_=ident[:].rearrange("q (i r) -> q i r", r=PARTITIONS_PER_NODE),
+            axis=mybir.AxisListType.X,
+        )
+        node_of = const.tile([P, NODES_PER_LOAD], BF16)
+        nc.vector.tensor_copy(out=node_of[:], in_=node_of_f32[:])
+
+        zero_col = const.tile([P, 1], F32)
+        nc.vector.memset(zero_col[:], 0.0)
+        half_col = const.tile([P, 1], F32)
+        nc.scalar.activation(out=half_col[:], in_=zero_col[:], func=ACT.Sigmoid)
+
+        gate_biases = ((bWi, bUi), (bWu, bUu), (bWo, bUo))
+        bias_rows = const.tile([P, P], BF16)
+        nc.vector.memset(bias_rows[:], 0.0)
+        rows_per_gate = PARTITIONS_PER_NODE * COL_TILES
+        for m, pair_of_biases in enumerate(gate_biases):
+            for r, b in enumerate(pair_of_biases):
+                nc.scalar.dma_start(
+                    out=bias_rows[rows_per_gate * m + r : rows_per_gate * (m + 1) : PARTITIONS_PER_NODE, :],
+                    in_=b.rearrange("(j p) -> j p", p=P),
+                )
+        bias_ps = psum.tile([P, NODES_PER_LOAD], F32, tag="bank")
+        nc.tensor.matmul(out=bias_ps[:], lhsT=bias_rows[:], rhs=node_of[:], start=True, stop=True)
+        bias = const.tile([P, NODES_PER_LOAD], F32)
+        nc.vector.tensor_copy(out=bias[:], in_=bias_ps[:])
+
+        def quantise_weight(w, label):
+            quantised = []
+            for g in range(PASSES):
+                raw = raw_pool.tile([P, PACK, HIDDEN], BF16)
+                nc.sync.dma_start(
+                    out=raw[:].rearrange("p (u e) n -> p u (e n)", u=2),
+                    in_=w[K_PASS * g : K_PASS * (g + 1), :].rearrange("(u p e) n -> p u (e n)", u=2, e=2),
+                )
+                grouped = grouped_pool.tile([P, HIDDEN, PACK], BF16, align_bytes=64)
+                for copy, cols in (
+                    (nc.vector.tensor_copy, slice(0, VECTOR_COLS)),
+                    (nc.scalar.copy, slice(VECTOR_COLS, HIDDEN)),
+                ):
+                    copy(
+                        out=grouped[:, cols, :].rearrange("p (c i) t -> p c t i", i=4),
+                        in_=raw[:, :, cols].rearrange("p t (c i) -> p c t i", i=4),
+                    )
+                words = keep.tile([P, HIDDEN], U32, align_bytes=64, name="words_%s%d" % (label, g))
+                scales = keep.tile([P, HIDDEN], U8, align_bytes=64, name="scales_%s%d" % (label, g))
+                nc.vector.quantize_mx(
+                    out=words[:].bitcast(FP8X4),
+                    scales=scales[:],
+                    in_=grouped[:].rearrange("p n t -> p (n t)"),
+                )
+                quantised.append((words, scales))
+            return quantised
+
+        def quantise_nodes(grouped, label):
+            words = keep.tile([P, PASSES, NODES], U32, align_bytes=64, name="words_" + label)
+            scales = keep.tile([P, PASSES, NODES], U8, align_bytes=64, name="scales_" + label)
+            nc.vector.quantize_mx(
+                out=words[:].rearrange("p g n -> p (g n)").bitcast(FP8X4),
+                scales=scales[:].rearrange("p g n -> p (g n)"),
+                in_=grouped[:].rearrange("p g n t -> p (g n t)"),
+            )
+            return words, scales
+
+        def gate(m, w_q, u_q, func, label):
+            result = keep.tile([P, COL_TILES, NODES], F32, name="gate_" + label)
+            acc = [psum.tile([P, NODES], F32, tag="bank", name="acc%d" % j) for j in range(COL_TILES)]
+            passes = [(w_q[g], x_q, g) for g in range(PASSES)] + [(u_q[g], h_q, g) for g in range(PASSES)]
+            for n, ((w_words, w_scales), (a_words, a_scales), g) in enumerate(passes):
+                for j in range(COL_TILES):
+                    cols = slice(P * j, P * (j + 1))
+                    nc.tensor.matmul_mx(
+                        out=acc[j][:],
+                        lhsT=w_words[:, cols].bitcast(FP8X4),
+                        lhsT_scale=w_scales[:, cols],
+                        rhs=a_words[:, g, :].bitcast(FP8X4),
+                        rhs_scale=a_scales[:, g, :],
+                        start=(n == 0),
+                        stop=(n == len(passes) - 1),
+                    )
+            for j in range(COL_TILES):
+                nc.scalar.activation(
+                    out=result[:, j, :],
+                    in_=acc[j][:],
+                    func=func,
+                    bias=bias[:, COL_TILES * m + j : COL_TILES * m + j + 1],
+                )
+            return result
+
+        def flip_back(source, a, half):
+            flipped = psum.tile([P, BANK], F32, tag="bank")
+            for q in range(BANK // P):
+                nc.tensor.transpose(
+                    flipped[:, P * q : P * (q + 1)],
+                    source[:, (BANK // P) * half + q, P * a : P * (a + 1)],
+                    ident[:],
+                )
+            return flipped
+
+        wi_q = quantise_weight(Wi, "wi")
+
+        x_sb = keep.tile([P, NODE_TILES, FEATURES], BF16)
+        nc.sync.dma_start(out=x_sb[:], in_=x.rearrange("(a p) k -> p a k", p=P))
+        x_words = x_sb[:].bitcast(F32)
+        x_grouped = keep.tile([P, PASSES, NODES, PACK], BF16, align_bytes=64)
+        for g in range(PASSES):
+            x_ps = psum.tile([P, 2, NODES], F32, tag="bank")
+            for u in range(2):
+                for a in range(NODE_TILES):
+                    first = (K_PASS // 2) * g + P * u
+                    nc.tensor.transpose(
+                        x_ps[:, u, P * a : P * (a + 1)], x_words[:, a, first : first + P], ident[:]
+                    )
+            nc.vector.tensor_copy(
+                out=x_grouped[:, g, :, :].bitcast(F32), in_=x_ps[:].rearrange("p u n -> p n u")
+            )
+        x_q = quantise_nodes(x_grouped, "x")
+
+        ui_q = quantise_weight(Ui, "ui")
+        wu_q = quantise_weight(Wu, "wu")
+
+        child_rows = child_h.rearrange("n c k -> (n c) k").rearrange(
+            "(l q s) k -> l q s k", q=P, s=ROWS_PER_PARTITION
+        )
+        loads_per_tile = CHILD_LOADS // NODE_TILES
+        h_grouped = keep.tile([P, PASSES, NODES, PACK], BF16, align_bytes=64)
+        for a in range(NODE_TILES):
+            h_ps = [
+                psum.tile([P, PACK, P], F32, tag="bank", name="h_ps%d" % g) for g in range(PASSES)
+            ]
+            for l in range(loads_per_tile):
+                child = child_pool.tile([P, ROWS_PER_PARTITION, FEATURES], BF16)
+                nc.sync.dma_start(out=child[:], in_=child_rows[loads_per_tile * a + l])
+                by_word = child[:].rearrange("q s (g u p e) -> q s g u e p", g=PASSES, u=2, e=2)
+                for g in range(PASSES):
+                    for t in range(PACK):
+                        for s in range(ROWS_PER_PARTITION):
+                            nc.tensor.matmul(
+                                out=h_ps[g][:, t, NODES_PER_LOAD * l : NODES_PER_LOAD * (l + 1)],
+                                lhsT=by_word[:, s, g, t // 2, t % 2, :],
+                                rhs=node_of[:],
+                                start=(s == 0),
+                                stop=(s == ROWS_PER_PARTITION - 1),
+                            )
+            for g, copy in enumerate((nc.vector.tensor_copy, nc.scalar.copy)):
+                copy(
+                    out=h_grouped[:, g, P * a : P * (a + 1), :],
+                    in_=h_ps[g][:].rearrange("p t n -> p n t"),
+                )
+        h_q = quantise_nodes(h_grouped, "h")
+
+        uu_q = quantise_weight(Uu, "uu")
+        fc_sb = keep.tile([P, NODE_TILES, HIDDEN], BF16)
+        nc.sync.dma_start(out=fc_sb[:], in_=fc_sum.rearrange("(a p) n -> p a n", p=P))
+
+        i_gate = gate(GATE_I, wi_q, ui_q, ACT.Sigmoid, "i")
+        u_gate = gate(GATE_U, wu_q, uu_q, ACT.Tanh, "u")
+        iu = keep.tile([P, COL_TILES, NODES], F32)
+        c_sb = keep.tile([P, NODE_TILES, HIDDEN], F32)
+        tanh_c = keep.tile([P, NODE_TILES, HIDDEN], F32)
+        for half in range(HIDDEN // BANK):
+            tiles = slice((BANK // P) * half, (BANK // P) * (half + 1))
+            cols = slice(BANK * half, BANK * (half + 1))
+            nc.vector.tensor_tensor(
+                out=iu[:, tiles, :], in0=i_gate[:, tiles, :], in1=u_gate[:, tiles, :], op=ALU.mult
+            )
+            for a in range(NODE_TILES):
+                iu_flipped = flip_back(iu, a, half)
+                nc.vector.tensor_tensor(
+                    out=c_sb[:, a, cols], in0=iu_flipped[:], in1=fc_sb[:, a, cols], op=ALU.add
+                )
+                nc.scalar.activation(out=tanh_c[:, a, cols], in_=c_sb[:, a, cols], func=ACT.Tanh)
+                nc.sync.dma_start(out=out[1, P * a : P * (a + 1), cols], in_=c_sb[:, a, cols])
+
+        wo_q = quantise_weight(Wo, "wo")
+        uo_q = quantise_weight(Uo, "uo")
+        o_gate = gate(GATE_O, wo_q, uo_q, ACT.Sigmoid, "o")
+        h_sb = keep.tile([P, NODE_TILES, HIDDEN], F32)
+        for half in range(HIDDEN // BANK):
+            cols = slice(BANK * half, BANK * (half + 1))
+            for a in range(NODE_TILES):
+                o_flipped = flip_back(o_gate, a, half)
+                nc.vector.tensor_tensor(
+                    out=h_sb[:, a, cols], in0=o_flipped[:], in1=tanh_c[:, a, cols], op=ALU.mult
+                )
+                nc.sync.dma_start(out=out[0, P * a : P * (a + 1), cols], in_=h_sb[:, a, cols])

@@ -78,14 +78,18 @@ def tile_childsumtreelstmcell_pb_kernel(
         bias = const.tile([P, NODES_PER_LOAD], F32)
         nc.vector.tensor_copy(out=bias[:], in_=bias_ps[:])
 
-        def quantise_weight(w, label):
+        def quantise_weight(w, label, k_order):
             quantised = []
             for g in range(PASSES):
                 raw = raw_pool.tile([P, PACK, HIDDEN], BF16)
-                nc.sync.dma_start(
-                    out=raw[:].rearrange("p (u e) n -> p u (e n)", u=2),
-                    in_=w[K_PASS * g : K_PASS * (g + 1), :].rearrange("(u p e) n -> p u (e n)", u=2, e=2),
-                )
+                rows = w[K_PASS * g : K_PASS * (g + 1), :]
+                if k_order == "as x":
+                    nc.sync.dma_start(
+                        out=raw[:].rearrange("p (u e) n -> p u (e n)", u=2),
+                        in_=rows.rearrange("(u p e) n -> p u (e n)", u=2, e=2),
+                    )
+                else:
+                    nc.sync.dma_start(out=raw[:], in_=rows.rearrange("(t p) n -> p t n", p=P))
                 grouped = grouped_pool.tile([P, HIDDEN, PACK], BF16, align_bytes=64)
                 for copy, cols in (
                     (nc.vector.tensor_copy, slice(0, VECTOR_COLS)),
@@ -150,7 +154,7 @@ def tile_childsumtreelstmcell_pb_kernel(
                 )
             return flipped
 
-        wi_q = quantise_weight(Wi, "wi")
+        wi_q = quantise_weight(Wi, "wi", "as x")
 
         x_sb = keep.tile([P, NODE_TILES, FEATURES], BF16)
         nc.sync.dma_start(out=x_sb[:], in_=x.rearrange("(a p) k -> p a k", p=P))
@@ -169,8 +173,8 @@ def tile_childsumtreelstmcell_pb_kernel(
             )
         x_q = quantise_nodes(x_grouped, "x")
 
-        ui_q = quantise_weight(Ui, "ui")
-        wu_q = quantise_weight(Wu, "wu")
+        ui_q = quantise_weight(Ui, "ui", "as h_sum")
+        wu_q = quantise_weight(Wu, "wu", "as x")
 
         child_rows = child_h.rearrange("n c k -> (n c) k").rearrange(
             "(l q s) k -> l q s k", q=P, s=ROWS_PER_PARTITION
@@ -184,13 +188,13 @@ def tile_childsumtreelstmcell_pb_kernel(
             for l in range(loads_per_tile):
                 child = child_pool.tile([P, ROWS_PER_PARTITION, FEATURES], BF16)
                 nc.sync.dma_start(out=child[:], in_=child_rows[loads_per_tile * a + l])
-                by_word = child[:].rearrange("q s (g u p e) -> q s g u e p", g=PASSES, u=2, e=2)
                 for g in range(PASSES):
                     for t in range(PACK):
+                        first = K_PASS * g + P * t
                         for s in range(ROWS_PER_PARTITION):
                             nc.tensor.matmul(
                                 out=h_ps[g][:, t, NODES_PER_LOAD * l : NODES_PER_LOAD * (l + 1)],
-                                lhsT=by_word[:, s, g, t // 2, t % 2, :],
+                                lhsT=child[:, s, first : first + P],
                                 rhs=node_of[:],
                                 start=(s == 0),
                                 stop=(s == ROWS_PER_PARTITION - 1),
@@ -202,7 +206,7 @@ def tile_childsumtreelstmcell_pb_kernel(
                 )
         h_q = quantise_nodes(h_grouped, "h")
 
-        uu_q = quantise_weight(Uu, "uu")
+        uu_q = quantise_weight(Uu, "uu", "as h_sum")
         fc_sb = keep.tile([P, NODE_TILES, HIDDEN], BF16)
         nc.sync.dma_start(out=fc_sb[:], in_=fc_sum.rearrange("(a p) n -> p a n", p=P))
 
@@ -225,8 +229,8 @@ def tile_childsumtreelstmcell_pb_kernel(
                 nc.scalar.activation(out=tanh_c[:, a, cols], in_=c_sb[:, a, cols], func=ACT.Tanh)
                 nc.sync.dma_start(out=out[1, P * a : P * (a + 1), cols], in_=c_sb[:, a, cols])
 
-        wo_q = quantise_weight(Wo, "wo")
-        uo_q = quantise_weight(Uo, "uo")
+        wo_q = quantise_weight(Wo, "wo", "as x")
+        uo_q = quantise_weight(Uo, "uo", "as h_sum")
         o_gate = gate(GATE_O, wo_q, uo_q, ACT.Sigmoid, "o")
         h_sb = keep.tile([P, NODE_TILES, HIDDEN], F32)
         for half in range(HIDDEN // BANK):

@@ -23,7 +23,7 @@ HIDDEN = 1024
 COL_TILES = HIDDEN // P
 BANK = 512
 
-ROWS_PER_PARTITION = 2
+ROWS_PER_PARTITION = 4
 NODES_PER_LOAD = P * ROWS_PER_PARTITION // CHILDREN
 PARTITIONS_PER_NODE = P // NODES_PER_LOAD
 CHILD_LOADS = NODES // NODES_PER_LOAD
@@ -42,7 +42,7 @@ def tile_childsumtreelstmcell_pb_kernel(
     with ExitStack() as ctx:
         const = ctx.enter_context(tc.tile_pool(name="const", bufs=1))
         keep = ctx.enter_context(tc.tile_pool(name="keep", bufs=1))
-        raw_pool = ctx.enter_context(tc.tile_pool(name="raw", bufs=6))
+        raw_pool = ctx.enter_context(tc.tile_pool(name="raw", bufs=5))
         grouped_pool = ctx.enter_context(tc.tile_pool(name="grouped", bufs=3))
         child_pool = ctx.enter_context(tc.tile_pool(name="child", bufs=4))
         psum = ctx.enter_context(tc.psum_pool(name="psum", bufs=8))
@@ -78,18 +78,14 @@ def tile_childsumtreelstmcell_pb_kernel(
         bias = const.tile([P, NODES_PER_LOAD], F32)
         nc.vector.tensor_copy(out=bias[:], in_=bias_ps[:])
 
-        def quantise_weight(w, label, k_order):
+        def quantise_weight(w, label):
             quantised = []
             for g in range(PASSES):
                 raw = raw_pool.tile([P, PACK, HIDDEN], BF16)
-                rows = w[K_PASS * g : K_PASS * (g + 1), :]
-                if k_order == "as x":
-                    nc.sync.dma_start(
-                        out=raw[:].rearrange("p (u e) n -> p u (e n)", u=2),
-                        in_=rows.rearrange("(u p e) n -> p u (e n)", u=2, e=2),
-                    )
-                else:
-                    nc.sync.dma_start(out=raw[:], in_=rows.rearrange("(t p) n -> p t n", p=P))
+                nc.sync.dma_start(
+                    out=raw[:].rearrange("p (u e) n -> p u (e n)", u=2),
+                    in_=w[K_PASS * g : K_PASS * (g + 1), :].rearrange("(u p e) n -> p u (e n)", u=2, e=2),
+                )
                 grouped = grouped_pool.tile([P, HIDDEN, PACK], BF16, align_bytes=64)
                 for copy, cols in (
                     (nc.vector.tensor_copy, slice(0, VECTOR_COLS)),
@@ -101,11 +97,12 @@ def tile_childsumtreelstmcell_pb_kernel(
                     )
                 words = keep.tile([P, HIDDEN], U32, align_bytes=64, name="words_%s%d" % (label, g))
                 scales = keep.tile([P, HIDDEN], U8, align_bytes=64, name="scales_%s%d" % (label, g))
-                nc.vector.quantize_mx(
-                    out=words[:].bitcast(FP8X4),
-                    scales=scales[:],
-                    in_=grouped[:].rearrange("p n t -> p (n t)"),
-                )
+                for cols in (slice(0, HIDDEN // 2), slice(HIDDEN // 2, HIDDEN)):
+                    nc.vector.quantize_mx(
+                        out=words[:, cols].bitcast(FP8X4),
+                        scales=scales[:, cols],
+                        in_=grouped[:, cols, :].rearrange("p n t -> p (n t)"),
+                    )
                 quantised.append((words, scales))
             return quantised
 
@@ -122,20 +119,26 @@ def tile_childsumtreelstmcell_pb_kernel(
         def gate(m, w_q, u_q, func, label):
             result = keep.tile([P, COL_TILES, NODES], F32, name="gate_" + label)
             acc = [psum.tile([P, NODES], F32, tag="bank", name="acc%d" % j) for j in range(COL_TILES)]
-            passes = [(w_q[g], x_q, g) for g in range(PASSES)] + [(u_q[g], h_q, g) for g in range(PASSES)]
-            for n, ((w_words, w_scales), (a_words, a_scales), g) in enumerate(passes):
+
+            def mx_pass(j, weight_q, nodes_q, g, start, stop):
+                (w_words, w_scales), (a_words, a_scales) = weight_q[g], nodes_q
+                cols = slice(P * j, P * (j + 1))
+                nc.tensor.matmul_mx(
+                    out=acc[j][:],
+                    lhsT=w_words[:, cols].bitcast(FP8X4),
+                    lhsT_scale=w_scales[:, cols],
+                    rhs=a_words[:, g, :].bitcast(FP8X4),
+                    rhs_scale=a_scales[:, g, :],
+                    start=start,
+                    stop=stop,
+                )
+
+            for g in range(PASSES):
                 for j in range(COL_TILES):
-                    cols = slice(P * j, P * (j + 1))
-                    nc.tensor.matmul_mx(
-                        out=acc[j][:],
-                        lhsT=w_words[:, cols].bitcast(FP8X4),
-                        lhsT_scale=w_scales[:, cols],
-                        rhs=a_words[:, g, :].bitcast(FP8X4),
-                        rhs_scale=a_scales[:, g, :],
-                        start=(n == 0),
-                        stop=(n == len(passes) - 1),
-                    )
+                    mx_pass(j, w_q, x_q, g, g == 0, False)
             for j in range(COL_TILES):
+                for g in range(PASSES):
+                    mx_pass(j, u_q, h_q, g, False, g == PASSES - 1)
                 nc.scalar.activation(
                     out=result[:, j, :],
                     in_=acc[j][:],
@@ -144,17 +147,18 @@ def tile_childsumtreelstmcell_pb_kernel(
                 )
             return result
 
-        def flip_back(source, a, half):
-            flipped = psum.tile([P, BANK], F32, tag="bank")
+        def flip_back(source, half):
+            flipped = [psum.tile([P, BANK], F32, tag="bank", name="flipped%d" % a) for a in range(NODE_TILES)]
             for q in range(BANK // P):
-                nc.tensor.transpose(
-                    flipped[:, P * q : P * (q + 1)],
-                    source[:, (BANK // P) * half + q, P * a : P * (a + 1)],
-                    ident[:],
-                )
+                for a in range(NODE_TILES):
+                    nc.tensor.transpose(
+                        flipped[a][:, P * q : P * (q + 1)],
+                        source[:, (BANK // P) * half + q, P * a : P * (a + 1)],
+                        ident[:],
+                    )
             return flipped
 
-        wi_q = quantise_weight(Wi, "wi", "as x")
+        wi_q = quantise_weight(Wi, "wi")
 
         x_sb = keep.tile([P, NODE_TILES, FEATURES], BF16)
         nc.sync.dma_start(out=x_sb[:], in_=x.rearrange("(a p) k -> p a k", p=P))
@@ -173,8 +177,8 @@ def tile_childsumtreelstmcell_pb_kernel(
             )
         x_q = quantise_nodes(x_grouped, "x")
 
-        ui_q = quantise_weight(Ui, "ui", "as h_sum")
-        wu_q = quantise_weight(Wu, "wu", "as x")
+        ui_q = quantise_weight(Ui, "ui")
+        wu_q = quantise_weight(Wu, "wu")
 
         child_rows = child_h.rearrange("n c k -> (n c) k").rearrange(
             "(l q s) k -> l q s k", q=P, s=ROWS_PER_PARTITION
@@ -188,25 +192,25 @@ def tile_childsumtreelstmcell_pb_kernel(
             for l in range(loads_per_tile):
                 child = child_pool.tile([P, ROWS_PER_PARTITION, FEATURES], BF16)
                 nc.sync.dma_start(out=child[:], in_=child_rows[loads_per_tile * a + l])
+                by_word = child[:].rearrange("q s (g u p e) -> q s g u e p", g=PASSES, u=2, e=2)
                 for g in range(PASSES):
                     for t in range(PACK):
-                        first = K_PASS * g + P * t
                         for s in range(ROWS_PER_PARTITION):
                             nc.tensor.matmul(
                                 out=h_ps[g][:, t, NODES_PER_LOAD * l : NODES_PER_LOAD * (l + 1)],
-                                lhsT=child[:, s, first : first + P],
+                                lhsT=by_word[:, s, g, t // 2, t % 2, :],
                                 rhs=node_of[:],
                                 start=(s == 0),
                                 stop=(s == ROWS_PER_PARTITION - 1),
                             )
-            for g, copy in enumerate((nc.vector.tensor_copy, nc.scalar.copy)):
-                copy(
+            for g in range(PASSES):
+                nc.vector.tensor_copy(
                     out=h_grouped[:, g, P * a : P * (a + 1), :],
                     in_=h_ps[g][:].rearrange("p t n -> p n t"),
                 )
         h_q = quantise_nodes(h_grouped, "h")
 
-        uu_q = quantise_weight(Uu, "uu", "as h_sum")
+        uu_q = quantise_weight(Uu, "uu")
         fc_sb = keep.tile([P, NODE_TILES, HIDDEN], BF16)
         nc.sync.dma_start(out=fc_sb[:], in_=fc_sum.rearrange("(a p) n -> p a n", p=P))
 
@@ -221,23 +225,23 @@ def tile_childsumtreelstmcell_pb_kernel(
             nc.vector.tensor_tensor(
                 out=iu[:, tiles, :], in0=i_gate[:, tiles, :], in1=u_gate[:, tiles, :], op=ALU.mult
             )
+            iu_flipped = flip_back(iu, half)
             for a in range(NODE_TILES):
-                iu_flipped = flip_back(iu, a, half)
                 nc.vector.tensor_tensor(
-                    out=c_sb[:, a, cols], in0=iu_flipped[:], in1=fc_sb[:, a, cols], op=ALU.add
+                    out=c_sb[:, a, cols], in0=iu_flipped[a][:], in1=fc_sb[:, a, cols], op=ALU.add
                 )
                 nc.scalar.activation(out=tanh_c[:, a, cols], in_=c_sb[:, a, cols], func=ACT.Tanh)
                 nc.sync.dma_start(out=out[1, P * a : P * (a + 1), cols], in_=c_sb[:, a, cols])
 
-        wo_q = quantise_weight(Wo, "wo", "as x")
-        uo_q = quantise_weight(Uo, "uo", "as h_sum")
+        wo_q = quantise_weight(Wo, "wo")
+        uo_q = quantise_weight(Uo, "uo")
         o_gate = gate(GATE_O, wo_q, uo_q, ACT.Sigmoid, "o")
         h_sb = keep.tile([P, NODE_TILES, HIDDEN], F32)
         for half in range(HIDDEN // BANK):
             cols = slice(BANK * half, BANK * (half + 1))
+            o_flipped = flip_back(o_gate, half)
             for a in range(NODE_TILES):
-                o_flipped = flip_back(o_gate, a, half)
                 nc.vector.tensor_tensor(
-                    out=h_sb[:, a, cols], in0=o_flipped[:], in1=tanh_c[:, a, cols], op=ALU.mult
+                    out=h_sb[:, a, cols], in0=o_flipped[a][:], in1=tanh_c[:, a, cols], op=ALU.mult
                 )
                 nc.sync.dma_start(out=out[0, P * a : P * (a + 1), cols], in_=h_sb[:, a, cols])

@@ -21,7 +21,10 @@ FEATURES = 1024
 PASSES = FEATURES // K_PASS
 HIDDEN = 1024
 COL_TILES = HIDDEN // P
+PSUM_BANKS = 8
 BANK = 512
+TILES_PER_BANK = BANK // P
+HALVES = HIDDEN // BANK
 
 ROWS_PER_PARTITION = 4
 NODES_PER_LOAD = P * ROWS_PER_PARTITION // CHILDREN
@@ -44,8 +47,8 @@ def tile_childsumtreelstmcell_pb_kernel(
         keep = ctx.enter_context(tc.tile_pool(name="keep", bufs=1))
         raw_pool = ctx.enter_context(tc.tile_pool(name="raw", bufs=5))
         grouped_pool = ctx.enter_context(tc.tile_pool(name="grouped", bufs=3))
-        child_pool = ctx.enter_context(tc.tile_pool(name="child", bufs=4))
-        psum = ctx.enter_context(tc.psum_pool(name="psum", bufs=8))
+        child_pool = ctx.enter_context(tc.tile_pool(name="child", bufs=CHILD_LOADS))
+        psum = ctx.enter_context(tc.psum_pool(name="psum", bufs=PSUM_BANKS))
 
         ident = const.tile([P, P], F32)
         make_identity(nc, ident[:])
@@ -58,10 +61,10 @@ def tile_childsumtreelstmcell_pb_kernel(
         node_of = const.tile([P, NODES_PER_LOAD], BF16)
         nc.vector.tensor_copy(out=node_of[:], in_=node_of_f32[:])
 
-        zero_col = const.tile([P, 1], F32)
-        nc.vector.memset(zero_col[:], 0.0)
-        half_col = const.tile([P, 1], F32)
-        nc.scalar.activation(out=half_col[:], in_=zero_col[:], func=ACT.Sigmoid)
+        table_in = const.tile([P, 1], F32)
+        nc.vector.memset(table_in[:], 0.0)
+        table_out = const.tile([P, 1], F32)
+        nc.scalar.activation(out=table_out[:], in_=table_in[:], func=ACT.Sigmoid)
 
         gate_biases = ((bWi, bUi), (bWu, bUu), (bWo, bUo))
         bias_rows = const.tile([P, P], BF16)
@@ -77,6 +80,7 @@ def tile_childsumtreelstmcell_pb_kernel(
         nc.tensor.matmul(out=bias_ps[:], lhsT=bias_rows[:], rhs=node_of[:], start=True, stop=True)
         bias = const.tile([P, NODES_PER_LOAD], F32)
         nc.vector.tensor_copy(out=bias[:], in_=bias_ps[:])
+
 
         def quantise_weight(w, label):
             quantised = []
@@ -121,14 +125,14 @@ def tile_childsumtreelstmcell_pb_kernel(
             acc = [psum.tile([P, NODES], F32, tag="bank", name="acc%d" % j) for j in range(COL_TILES)]
 
             def mx_pass(j, weight_q, nodes_q, g, start, stop):
-                (w_words, w_scales), (a_words, a_scales) = weight_q[g], nodes_q
+                (w_words, w_scales), (n_words, n_scales) = weight_q[g], nodes_q
                 cols = slice(P * j, P * (j + 1))
                 nc.tensor.matmul_mx(
                     out=acc[j][:],
                     lhsT=w_words[:, cols].bitcast(FP8X4),
                     lhsT_scale=w_scales[:, cols],
-                    rhs=a_words[:, g, :].bitcast(FP8X4),
-                    rhs_scale=a_scales[:, g, :],
+                    rhs=n_words[:, g, :].bitcast(FP8X4),
+                    rhs_scale=n_scales[:, g, :],
                     start=start,
                     stop=stop,
                 )
@@ -138,7 +142,7 @@ def tile_childsumtreelstmcell_pb_kernel(
                     mx_pass(j, w_q, x_q, g, g == 0, False)
             for j in range(COL_TILES):
                 for g in range(PASSES):
-                    mx_pass(j, u_q, h_q, g, False, g == PASSES - 1)
+                    mx_pass(j, u_q, hsum_q, g, False, g == PASSES - 1)
                 nc.scalar.activation(
                     out=result[:, j, :],
                     in_=acc[j][:],
@@ -149,11 +153,11 @@ def tile_childsumtreelstmcell_pb_kernel(
 
         def flip_back(source, half):
             flipped = [psum.tile([P, BANK], F32, tag="bank", name="flipped%d" % a) for a in range(NODE_TILES)]
-            for q in range(BANK // P):
+            for q in range(TILES_PER_BANK):
                 for a in range(NODE_TILES):
                     nc.tensor.transpose(
                         flipped[a][:, P * q : P * (q + 1)],
-                        source[:, (BANK // P) * half + q, P * a : P * (a + 1)],
+                        source[:, TILES_PER_BANK * half + q, P * a : P * (a + 1)],
                         ident[:],
                     )
             return flipped
@@ -162,7 +166,7 @@ def tile_childsumtreelstmcell_pb_kernel(
 
         x_sb = keep.tile([P, NODE_TILES, FEATURES], BF16)
         nc.sync.dma_start(out=x_sb[:], in_=x.rearrange("(a p) k -> p a k", p=P))
-        x_words = x_sb[:].bitcast(F32)
+        x_pairs = x_sb[:].bitcast(F32)
         x_grouped = keep.tile([P, PASSES, NODES, PACK], BF16, align_bytes=64)
         for g in range(PASSES):
             x_ps = psum.tile([P, 2, NODES], F32, tag="bank")
@@ -170,7 +174,7 @@ def tile_childsumtreelstmcell_pb_kernel(
                 for a in range(NODE_TILES):
                     first = (K_PASS // 2) * g + P * u
                     nc.tensor.transpose(
-                        x_ps[:, u, P * a : P * (a + 1)], x_words[:, a, first : first + P], ident[:]
+                        x_ps[:, u, P * a : P * (a + 1)], x_pairs[:, a, first : first + P], ident[:]
                     )
             nc.vector.tensor_copy(
                 out=x_grouped[:, g, :, :].bitcast(F32), in_=x_ps[:].rearrange("p u n -> p n u")
@@ -184,31 +188,31 @@ def tile_childsumtreelstmcell_pb_kernel(
             "(l q s) k -> l q s k", q=P, s=ROWS_PER_PARTITION
         )
         loads_per_tile = CHILD_LOADS // NODE_TILES
-        h_grouped = keep.tile([P, PASSES, NODES, PACK], BF16, align_bytes=64)
+        hsum_grouped = keep.tile([P, PASSES, NODES, PACK], BF16, align_bytes=64)
         for a in range(NODE_TILES):
-            h_ps = [
-                psum.tile([P, PACK, P], F32, tag="bank", name="h_ps%d" % g) for g in range(PASSES)
+            hsum_ps = [
+                psum.tile([P, PACK, P], F32, tag="bank", name="hsum_ps%d" % g) for g in range(PASSES)
             ]
             for l in range(loads_per_tile):
                 child = child_pool.tile([P, ROWS_PER_PARTITION, FEATURES], BF16)
                 nc.sync.dma_start(out=child[:], in_=child_rows[loads_per_tile * a + l])
-                by_word = child[:].rearrange("q s (g u p e) -> q s g u e p", g=PASSES, u=2, e=2)
+                child_k = child[:].rearrange("q s (g u p e) -> q s g u e p", g=PASSES, u=2, e=2)
                 for g in range(PASSES):
                     for t in range(PACK):
                         for s in range(ROWS_PER_PARTITION):
                             nc.tensor.matmul(
-                                out=h_ps[g][:, t, NODES_PER_LOAD * l : NODES_PER_LOAD * (l + 1)],
-                                lhsT=by_word[:, s, g, t // 2, t % 2, :],
+                                out=hsum_ps[g][:, t, NODES_PER_LOAD * l : NODES_PER_LOAD * (l + 1)],
+                                lhsT=child_k[:, s, g, t // 2, t % 2, :],
                                 rhs=node_of[:],
                                 start=(s == 0),
                                 stop=(s == ROWS_PER_PARTITION - 1),
                             )
             for g in range(PASSES):
                 nc.vector.tensor_copy(
-                    out=h_grouped[:, g, P * a : P * (a + 1), :],
-                    in_=h_ps[g][:].rearrange("p t n -> p n t"),
+                    out=hsum_grouped[:, g, P * a : P * (a + 1), :],
+                    in_=hsum_ps[g][:].rearrange("p t n -> p n t"),
                 )
-        h_q = quantise_nodes(h_grouped, "h")
+        hsum_q = quantise_nodes(hsum_grouped, "hsum")
 
         uu_q = quantise_weight(Uu, "uu")
         fc_sb = keep.tile([P, NODE_TILES, HIDDEN], BF16)
@@ -219,8 +223,8 @@ def tile_childsumtreelstmcell_pb_kernel(
         iu = keep.tile([P, COL_TILES, NODES], F32)
         c_sb = keep.tile([P, NODE_TILES, HIDDEN], F32)
         tanh_c = keep.tile([P, NODE_TILES, HIDDEN], F32)
-        for half in range(HIDDEN // BANK):
-            tiles = slice((BANK // P) * half, (BANK // P) * (half + 1))
+        for half in range(HALVES):
+            tiles = slice(TILES_PER_BANK * half, TILES_PER_BANK * (half + 1))
             cols = slice(BANK * half, BANK * (half + 1))
             nc.vector.tensor_tensor(
                 out=iu[:, tiles, :], in0=i_gate[:, tiles, :], in1=u_gate[:, tiles, :], op=ALU.mult
@@ -237,7 +241,7 @@ def tile_childsumtreelstmcell_pb_kernel(
         uo_q = quantise_weight(Uo, "uo")
         o_gate = gate(GATE_O, wo_q, uo_q, ACT.Sigmoid, "o")
         h_sb = keep.tile([P, NODE_TILES, HIDDEN], F32)
-        for half in range(HIDDEN // BANK):
+        for half in range(HALVES):
             cols = slice(BANK * half, BANK * (half + 1))
             o_flipped = flip_back(o_gate, half)
             for a in range(NODE_TILES):

from contextlib import ExitStack

import concourse.mybir as mybir
from concourse.masks import make_identity

F32 = mybir.dt.float32
BF16 = mybir.dt.bfloat16
U32 = mybir.dt.uint32
U8 = mybir.dt.uint8
FP8X4 = mybir.dt.float8_e4m3fn_x4
ACT = mybir.ActivationFunctionType
ALU = mybir.AluOpType

P = 128
PACK = 4
K_PASS = P * PACK
NODES = 256
NODE_TILES = NODES // P
CHILDREN = 8
FEATURES = 1024
PASSES = FEATURES // K_PASS
HIDDEN = 1024
COL_TILES = HIDDEN // P
PSUM_BANKS = 8
BANK = 512
TILES_PER_BANK = BANK // P
HALVES = HIDDEN // BANK

ROWS_PER_PARTITION = 4
NODES_PER_LOAD = P * ROWS_PER_PARTITION // CHILDREN
PARTITIONS_PER_NODE = P // NODES_PER_LOAD
CHILD_LOADS = NODES // NODES_PER_LOAD

GATE_I, GATE_U, GATE_O = 0, 1, 2

VECTOR_COLS = 512

FLOPS = 2 * NODES * FEATURES * HIDDEN * 6


def tile_childsumtreelstmcell_pb_kernel(
    tc, x, child_h, fc_sum, Wi, bWi, Ui, bUi, Wo, bWo, Uo, bUo, Wu, bWu, Uu, bUu, out
):
    nc = tc.nc
    with ExitStack() as ctx:
        const = ctx.enter_context(tc.tile_pool(name="const", bufs=1))
        keep = ctx.enter_context(tc.tile_pool(name="keep", bufs=1))
        raw_pool = ctx.enter_context(tc.tile_pool(name="raw", bufs=5))
        grouped_pool = ctx.enter_context(tc.tile_pool(name="grouped", bufs=3))
        child_pool = ctx.enter_context(tc.tile_pool(name="child", bufs=CHILD_LOADS))
        psum = ctx.enter_context(tc.psum_pool(name="psum", bufs=PSUM_BANKS))

        ident = const.tile([P, P], F32)
        make_identity(nc, ident[:])
        node_of_f32 = const.tile([P, NODES_PER_LOAD], F32)
        nc.vector.reduce_sum(
            out=node_of_f32[:],
            in_=ident[:].rearrange("q (i r) -> q i r", r=PARTITIONS_PER_NODE),
            axis=mybir.AxisListType.X,
        )
        node_of = const.tile([P, NODES_PER_LOAD], BF16)
        nc.vector.tensor_copy(out=node_of[:], in_=node_of_f32[:])

        table_in = const.tile([P, 1], F32)
        nc.vector.memset(table_in[:], 0.0)
        table_out = const.tile([P, 1], F32)
        nc.scalar.activation(out=table_out[:], in_=table_in[:], func=ACT.Sigmoid)

        gate_biases = ((bWi, bUi), (bWu, bUu), (bWo, bUo))
        bias_rows = const.tile([P, P], BF16)
        nc.vector.memset(bias_rows[:], 0.0)
        rows_per_gate = PARTITIONS_PER_NODE * COL_TILES
        for m, pair_of_biases in enumerate(gate_biases):
            for r, b in enumerate(pair_of_biases):
                nc.scalar.dma_start(
                    out=bias_rows[rows_per_gate * m + r : rows_per_gate * (m + 1) : PARTITIONS_PER_NODE, :],
                    in_=b.rearrange("(j p) -> j p", p=P),
                )
        bias_ps = psum.tile([P, NODES_PER_LOAD], F32, tag="bank")
        nc.tensor.matmul(out=bias_ps[:], lhsT=bias_rows[:], rhs=node_of[:], start=True, stop=True)
        bias = const.tile([P, NODES_PER_LOAD], F32)
        nc.vector.tensor_copy(out=bias[:], in_=bias_ps[:])


        def quantise_weight(w, label):
            quantised = []
            for g in range(PASSES):
                raw = raw_pool.tile([P, PACK, HIDDEN], BF16)
                nc.sync.dma_start(
                    out=raw[:].rearrange("p (u e) n -> p u (e n)", u=2),
                    in_=w[K_PASS * g : K_PASS * (g + 1), :].rearrange("(u p e) n -> p u (e n)", u=2, e=2),
                )
                grouped = grouped_pool.tile([P, HIDDEN, PACK], BF16, align_bytes=64)
                for copy, cols in (
                    (nc.vector.tensor_copy, slice(0, VECTOR_COLS)),
                    (nc.scalar.copy, slice(VECTOR_COLS, HIDDEN)),
                ):
                    copy(
                        out=grouped[:, cols, :].rearrange("p (c i) t -> p c t i", i=4),
                        in_=raw[:, :, cols].rearrange("p t (c i) -> p c t i", i=4),
                    )
                words = keep.tile([P, HIDDEN], U32, align_bytes=64, name="words_%s%d" % (label, g))
                scales = keep.tile([P, HIDDEN], U8, align_bytes=64, name="scales_%s%d" % (label, g))
                for cols in (slice(0, HIDDEN // 2), slice(HIDDEN // 2, HIDDEN)):
                    nc.vector.quantize_mx(
                        out=words[:, cols].bitcast(FP8X4),
                        scales=scales[:, cols],
                        in_=grouped[:, cols, :].rearrange("p n t -> p (n t)"),
                    )
                quantised.append((words, scales))
            return quantised

        def quantise_nodes(grouped, label):
            words = keep.tile([P, PASSES, NODES], U32, align_bytes=64, name="words_" + label)
            scales = keep.tile([P, PASSES, NODES], U8, align_bytes=64, name="scales_" + label)
            nc.vector.quantize_mx(
                out=words[:].rearrange("p g n -> p (g n)").bitcast(FP8X4),
                scales=scales[:].rearrange("p g n -> p (g n)"),
                in_=grouped[:].rearrange("p g n t -> p (g n t)"),
            )
            return words, scales

        def gate(m, w_q, u_q, func, label):
            result = keep.tile([P, COL_TILES, NODES], F32, name="gate_" + label)
            acc = [psum.tile([P, NODES], F32, tag="bank", name="acc%d" % j) for j in range(COL_TILES)]

            def mx_pass(j, weight_q, nodes_q, g, start, stop):
                (w_words, w_scales), (n_words, n_scales) = weight_q[g], nodes_q
                cols = slice(P * j, P * (j + 1))
                nc.tensor.matmul_mx(
                    out=acc[j][:],
                    lhsT=w_words[:, cols].bitcast(FP8X4),
                    lhsT_scale=w_scales[:, cols],
                    rhs=n_words[:, g, :].bitcast(FP8X4),
                    rhs_scale=n_scales[:, g, :],
                    start=start,
                    stop=stop,
                )

            for g in range(PASSES):
                for j in range(COL_TILES):
                    mx_pass(j, w_q, x_q, g, g == 0, False)
            for j in range(COL_TILES):
                for g in range(PASSES):
                    mx_pass(j, u_q, hsum_q, g, False, g == PASSES - 1)
                nc.scalar.activation(
                    out=result[:, j, :],
                    in_=acc[j][:],
                    func=func,
                    bias=bias[:, COL_TILES * m + j : COL_TILES * m + j + 1],
                )
            return result

        def flip_back(source, half):
            flipped = [psum.tile([P, BANK], F32, tag="bank", name="flipped%d" % a) for a in range(NODE_TILES)]
            for q in range(TILES_PER_BANK):
                for a in range(NODE_TILES):
                    nc.tensor.transpose(
                        flipped[a][:, P * q : P * (q + 1)],
                        source[:, TILES_PER_BANK * half + q, P * a : P * (a + 1)],
                        ident[:],
                    )
            return flipped

        wi_q = quantise_weight(Wi, "wi")

        x_sb = keep.tile([P, NODE_TILES, FEATURES], BF16)
        nc.sync.dma_start(out=x_sb[:], in_=x.rearrange("(a p) k -> p a k", p=P))
        x_pairs = x_sb[:].bitcast(F32)
        x_grouped = keep.tile([P, PASSES, NODES, PACK], BF16, align_bytes=64)
        for g in range(PASSES):
            x_ps = psum.tile([P, 2, NODES], F32, tag="bank")
            for u in range(2):
                for a in range(NODE_TILES):
                    first = (K_PASS // 2) * g + P * u
                    nc.tensor.transpose(
                        x_ps[:, u, P * a : P * (a + 1)], x_pairs[:, a, first : first + P], ident[:]
                    )
            nc.vector.tensor_copy(
                out=x_grouped[:, g, :, :].bitcast(F32), in_=x_ps[:].rearrange("p u n -> p n u")
            )
        x_q = quantise_nodes(x_grouped, "x")

        ui_q = quantise_weight(Ui, "ui")
        wu_q = quantise_weight(Wu, "wu")

        child_rows = child_h.rearrange("n c k -> (n c) k").rearrange(
            "(l q s) k -> l q s k", q=P, s=ROWS_PER_PARTITION
        )
        loads_per_tile = CHILD_LOADS // NODE_TILES
        hsum_grouped = keep.tile([P, PASSES, NODES, PACK], BF16, align_bytes=64)
        for a in range(NODE_TILES):
            hsum_ps = [
                psum.tile([P, PACK, P], F32, tag="bank", name="hsum_ps%d" % g) for g in range(PASSES)
            ]
            for l in range(loads_per_tile):
                child = child_pool.tile([P, ROWS_PER_PARTITION, FEATURES], BF16)
                nc.sync.dma_start(out=child[:], in_=child_rows[loads_per_tile * a + l])
                child_k = child[:].rearrange("q s (g u p e) -> q s g u e p", g=PASSES, u=2, e=2)
                for g in range(PASSES):
                    for t in range(PACK):
                        for s in range(ROWS_PER_PARTITION):
                            nc.tensor.matmul(
                                out=hsum_ps[g][:, t, NODES_PER_LOAD * l : NODES_PER_LOAD * (l + 1)],
                                lhsT=child_k[:, s, g, t // 2, t % 2, :],
                                rhs=node_of[:],
                                start=(s == 0),
                                stop=(s == ROWS_PER_PARTITION - 1),
                            )
            for g in range(PASSES):
                nc.vector.tensor_copy(
                    out=hsum_grouped[:, g, P * a : P * (a + 1), :],
                    in_=hsum_ps[g][:].rearrange("p t n -> p n t"),
                )
        hsum_q = quantise_nodes(hsum_grouped, "hsum")

        uu_q = quantise_weight(Uu, "uu")
        fc_sb = keep.tile([P, NODE_TILES, HIDDEN], BF16)
        nc.sync.dma_start(out=fc_sb[:], in_=fc_sum.rearrange("(a p) n -> p a n", p=P))

        i_gate = gate(GATE_I, wi_q, ui_q, ACT.Sigmoid, "i")
        u_gate = gate(GATE_U, wu_q, uu_q, ACT.Tanh, "u")
        iu = keep.tile([P, COL_TILES, NODES], F32)
        c_sb = keep.tile([P, NODE_TILES, HIDDEN], F32)
        tanh_c = keep.tile([P, NODE_TILES, HIDDEN], F32)
        for half in range(HALVES):
            tiles = slice(TILES_PER_BANK * half, TILES_PER_BANK * (half + 1))
            cols = slice(BANK * half, BANK * (half + 1))
            nc.vector.tensor_tensor(
                out=iu[:, tiles, :], in0=i_gate[:, tiles, :], in1=u_gate[:, tiles, :], op=ALU.mult
            )
            iu_flipped = flip_back(iu, half)
            for a in range(NODE_TILES):
                nc.vector.tensor_tensor(
                    out=c_sb[:, a, cols], in0=iu_flipped[a][:], in1=fc_sb[:, a, cols], op=ALU.add
                )
                nc.scalar.activation(out=tanh_c[:, a, cols], in_=c_sb[:, a, cols], func=ACT.Tanh)
                nc.sync.dma_start(out=out[1, P * a : P * (a + 1), cols], in_=c_sb[:, a, cols])

        wo_q = quantise_weight(Wo, "wo")
        uo_q = quantise_weight(Uo, "uo")
        o_gate = gate(GATE_O, wo_q, uo_q, ACT.Sigmoid, "o")
        h_sb = keep.tile([P, NODE_TILES, HIDDEN], F32)
        for half in range(HALVES):
            cols = slice(BANK * half, BANK * (half + 1))
            o_flipped = flip_back(o_gate, half)
            for a in range(NODE_TILES):
                nc.vector.tensor_tensor(
                    out=h_sb[:, a, cols], in0=o_flipped[a][:], in1=tanh_c[:, a, cols], op=ALU.mult
                )
                nc.sync.dma_start(out=out[0, P * a : P * (a + 1), cols], in_=h_sb[:, a, cols])
